import numpy as np
import ml_dtypes


def mxq(x, axis, fmt="e4m3"):
    dtype, down = {"e4m3": (ml_dtypes.float8_e4m3fn, 7), "e5m2": (ml_dtypes.float8_e5m2, 14)}[fmt]
    v = np.moveaxis(np.asarray(x, np.float32).astype(ml_dtypes.bfloat16).astype(np.float64), axis, -1)
    blocks = v.reshape(v.shape[:-1] + (-1, 32))
    amax = np.abs(blocks).max(-1, keepdims=True)
    byte = np.maximum(np.where(amax > 0, np.frexp(amax)[1] - 1 + 127, 0) - down, 1)
    scale = np.exp2(byte - 127.0)
    codes = (blocks / scale).astype(np.float32).astype(dtype).astype(np.float64)
    return np.moveaxis((codes * scale).reshape(v.shape), -1, axis)


WIDE = False


def mx_kscale(k):
    if not WIDE:
        return np.ones(k)
    levels = np.array([10, -10, 5, -5, 0])
    a = np.random.permutation(np.resize(levels, k // 512 * 4)).reshape(k // 512, 4)
    idx = np.arange(k)
    return np.exp2(a[idx // 512, idx % 128 // 32])


BF16 = ml_dtypes.bfloat16


def bf(x):
    return np.asarray(x, np.float32).astype(BF16)


def f64(x):
    return np.asarray(x).astype(np.float64)


B, T, C, H = 2, 512, 1024, 8
DH = C // H


def rope_tables():
    i = f64(np.arange(1, DH // 2 + 1))
    thetas = np.repeat(1000.0 ** (-2.0 * i / DH), 2)
    pos = f64(np.arange(1, T + 1))
    args = pos[:, None] * thetas[None, :]
    return np.sin(args), np.cos(args)


def apply_rope(u, sin, cos):
    u_odd = u[..., ::2]
    u_even = u[..., 1::2]
    u_sin = np.stack([-u_even, u_odd], axis=-1).reshape(u.shape)
    return u * cos + u_sin * sin


def setup_inputs():
    s = mx_kscale(C)
    return {"x": bf(np.random.standard_normal((B, T, C)) * s),
            "w_qk": bf(np.random.standard_normal((2 * C, C)) / np.sqrt(C) / s[None, :])}


def reference(x, w_qk):
    qk = mxq(f64(x), 2, "e4m3") @ mxq(f64(w_qk), 1, "e4m3").T
    q, k = np.split(qk, 2, axis=-1)
    q = q.reshape(B, T, H, DH).transpose(0, 2, 1, 3)
    k = k.reshape(B, T, H, DH).transpose(0, 2, 1, 3)
    sin, cos = rope_tables()
    return q, k, apply_rope(q, sin, cos), apply_rope(k, sin, cos)

@@ -1,0 +1,213 @@
+import math
+from contextlib import ExitStack
+
+import concourse.masks as masks
+import concourse.mybir as mybir
+
+F32 = mybir.dt.float32
+BF16 = mybir.dt.bfloat16
+I32 = mybir.dt.int32
+U32 = mybir.dt.uint32
+U8 = mybir.dt.uint8
+FP8X4 = mybir.dt.float8_e4m3fn_x4
+ALU = mybir.AluOpType
+ACT = mybir.ActivationFunctionType
+
+B, T, C, H, DH = 2, 512, 1024, 8, 128
+P = 128
+PACK = 4
+PASSES = C // (P * PACK)
+J = T // P
+CHUNK = 512
+CHUNKS = 2 * C // CHUNK
+ROW_TILES = CHUNK // P
+HEADS = CHUNK // DH
+PAIRS = DH // 2
+
+FLOPS = 2 * B * T * C * 2 * C
+
+RATIO = 1000.0 ** (-2.0 / DH)
+ROUND_MAGIC = 1.5 * 2.0**23
+
+
+def tile_ropeattnlayer_pa_kernel(tc, x, w_qk, out_0, out_1, out_2, out_3):
+    nc = tc.nc
+    with ExitStack() as ctx:
+        const = ctx.enter_context(tc.tile_pool(name="const", bufs=1))
+        loaded = ctx.enter_context(tc.tile_pool(name="loaded", bufs=1))
+        keep = ctx.enter_context(tc.tile_pool(name="keep", bufs=1))
+        stage = ctx.enter_context(tc.tile_pool(name="stage", bufs=4))
+        results = ctx.enter_context(tc.tile_pool(name="results", bufs=3))
+        psum_flip = ctx.enter_context(tc.psum_pool(name="psum_flip", bufs=2))
+        psum_acc = ctx.enter_context(tc.psum_pool(name="psum_acc", bufs=6))
+
+        w_tiles = w_qk.rearrange("(c t p) k -> c t p k", t=ROW_TILES, p=P)
+        x_tiles = x.rearrange("b (p j) k -> b j p k", j=J)
+        w_rows = [[None] * ROW_TILES for c in range(CHUNKS)]
+        x_rows = [[None] * J for b in range(B)]
+
+        def load_w(c):
+            for t in range(ROW_TILES):
+                w_rows[c][t] = loaded.tile([P, C], BF16, name="w_rows%d_%d" % (c, t))
+                nc.sync.dma_start(out=w_rows[c][t][:], in_=w_tiles[c, t])
+
+        def load_x(b):
+            for j in range(J):
+                x_rows[b][j] = loaded.tile([P, C], BF16, name="x_rows%d_%d" % (b, j))
+                nc.sync.dma_start(out=x_rows[b][j][:], in_=x_tiles[b, j])
+
+        load_w(0)
+        load_x(0)
+        for c in range(1, CHUNKS):
+            load_w(c)
+        load_x(1)
+
+        zero = const.tile([P, 1], F32)
+        nc.vector.memset(zero[:], 0.0)
+        warm = const.tile([P, 1], F32)
+        nc.scalar.activation(out=warm[:], in_=zero[:], func=ACT.Sin)
+
+        position_int = const.tile([P, J], I32)
+        nc.gpsimd.iota(position_int[:], pattern=[[1, J]], base=1, channel_multiplier=J)
+        ident = const.tile([P, P], F32)
+        masks.make_identity(nc, ident[:])
+        position = const.tile([P, J], F32)
+        nc.vector.tensor_copy(out=position[:], in_=position_int[:])
+        turns = const.tile([P, 2, J, PAIRS], F32)
+        nc.vector.tensor_scalar_mul(
+            out=turns[:, 1, :, 0:1], in0=position[:].unsqueeze(2), scalar1=RATIO / (2.0 * math.pi)
+        )
+        for doubling in range(6):
+            n = 2**doubling
+            nc.vector.tensor_scalar_mul(
+                out=turns[:, 1, :, n : 2 * n], in0=turns[:, 1, :, 0:n], scalar1=RATIO**n
+            )
+        nc.vector.tensor_scalar_add(out=turns[:, 0], in0=turns[:, 1], scalar1=0.25)
+        whole = const.tile([P, 2, J, PAIRS], F32)
+        nc.vector.tensor_scalar(
+            out=whole[:],
+            in0=turns[:],
+            scalar1=ROUND_MAGIC,
+            scalar2=ROUND_MAGIC,
+            op0=ALU.add,
+            op1=ALU.subtract,
+        )
+        part = const.tile([P, 2, J, PAIRS], F32)
+        nc.vector.tensor_sub(out=part[:], in0=turns[:], in1=whole[:])
+
+        table = const.tile([P, 2, J, DH], F32)
+
+        def fill_table():
+            cos_part = part[:, 0].rearrange("p j i -> p (j i)")
+            sin_part = part[:, 1].rearrange("p j i -> p (j i)")
+            cos_out = table[:, 0].rearrange("p j (i e) -> p (j i) e", e=2)
+            sin_out = table[:, 1].rearrange("p j (i e) -> p (j i) e", e=2)
+            nc.scalar.activation(
+                out=cos_out,
+                in_=cos_part.unsqueeze(2).to_broadcast([P, J * PAIRS, 2]),
+                func=ACT.Sin,
+                scale=2.0 * math.pi,
+            )
+            nc.scalar.activation(
+                out=sin_out[:, :, 0], in_=sin_part, func=ACT.Sin, scale=2.0 * math.pi
+            )
+            nc.scalar.activation(
+                out=sin_out[:, :, 1], in_=sin_part, func=ACT.Sin, scale=-2.0 * math.pi
+            )
+
+        x_codes = [
+            [keep.tile([P, PASSES, P], U32, name="x_codes%d_%d" % (b, j), align_bytes=64) for j in range(J)]
+            for b in range(B)
+        ]
+        x_scales = [
+            [keep.tile([P, PASSES, P], U8, name="x_scales%d_%d" % (b, j), align_bytes=64) for j in range(J)]
+            for b in range(B)
+        ]
+        w_codes = [
+            keep.tile([P, PASSES, CHUNK], U32, name="w_codes%d" % c, align_bytes=64) for c in range(CHUNKS)
+        ]
+        w_scales = [
+            keep.tile([P, PASSES, CHUNK], U8, name="w_scales%d" % c, align_bytes=64) for c in range(CHUNKS)
+        ]
+
+        def quantise_rows(rows, codes, scales):
+            words = rows[:].bitcast(F32)
+            flipped = psum_flip.tile([P, PASSES, 2, P], F32, tag="flipped")
+            for g in range(PASSES):
+                for u in range(2):
+                    first = (2 * g + u) * P
+                    nc.tensor.transpose(flipped[:, g, u, :], words[:, first : first + P], ident[:])
+            grouped = stage.tile([P, PASSES * P * PACK], BF16, tag="grouped", align_bytes=64)
+            nc.scalar.copy(
+                out=grouped[:].bitcast(F32).rearrange("p (g r u) -> p g r u", g=PASSES, u=2),
+                in_=flipped[:].rearrange("p g u r -> p g r u"),
+            )
+            for g in range(PASSES):
+                nc.vector.quantize_mx(
+                    out=codes[:, g, :].bitcast(FP8X4),
+                    scales=scales[:, g, :],
+                    in_=grouped[:, g * P * PACK : (g + 1) * P * PACK],
+                )
+
+        def quantise_x(b, j):
+            quantise_rows(x_rows[b][j], x_codes[b][j][:], x_scales[b][j][:])
+
+        def quantise_w(c, t):
+            columns = slice(t * P, (t + 1) * P)
+            quantise_rows(w_rows[c][t], w_codes[c][:, :, columns], w_scales[c][:, :, columns])
+
+        def project_and_rotate(b, c, j, plain, rotated):
+            acc = psum_acc.tile([P, CHUNK], F32, tag="acc")
+            for g in range(PASSES):
+                nc.tensor.matmul_mx(
+                    out=acc[:],
+                    lhsT=x_codes[b][j][:, g, :].bitcast(FP8X4),
+                    lhsT_scale=x_scales[b][j][:, g, :],
+                    rhs=w_codes[c][:, g, :].bitcast(FP8X4),
+                    rhs_scale=w_scales[c][:, g, :],
+                    start=(g == 0),
+                    stop=(g == PASSES - 1),
+                )
+            by_head = acc[:].rearrange("p (h d) -> p h d", h=HEADS)
+            products = stage.tile([P, 2, HEADS, DH], F32, tag="products")
+            nc.vector.tensor_tensor(
+                out=products[:],
+                in0=by_head.unsqueeze(1).to_broadcast([P, 2, HEADS, DH]),
+                in1=table[:, :, j, :].unsqueeze(2).to_broadcast([P, 2, HEADS, DH]),
+                op=ALU.mult,
+            )
+            nc.scalar.copy(out=plain[:, :, j, :], in_=by_head)
+            pairs = "p h (i e) -> p h i e"
+            nc.gpsimd.tensor_tensor(
+                out=rotated[:, :, j, :].rearrange(pairs, e=2),
+                in0=products[:, 0].rearrange(pairs, e=2),
+                in1=products[:, 1].rearrange(pairs, e=2)[:, :, :, ::-1],
+                op=ALU.add,
+            )
+
+        def store(result, out, b, first_head):
+            nc.sync.dma_start(
+                out=out[b, first_head : first_head + HEADS].rearrange("h (p j) d -> p h (j d)", j=J),
+                in_=result[:].rearrange("p h j d -> p h (j d)"),
+            )
+
+        for t in range(ROW_TILES):
+            quantise_w(0, t)
+        quantise_x(0, 0)
+        fill_table()
+        for b in range(B):
+            for c in range(CHUNKS):
+                plain = results.tile([P, HEADS, J, DH], F32, tag="plain")
+                rotated = results.tile([P, HEADS, J, DH], F32, tag="rotated")
+                for j in range(J):
+                    if b == 0 and c == 0 and j + 1 < J:
+                        quantise_x(0, j + 1)
+                    if b == 0 and c + 1 < CHUNKS:
+                        quantise_w(c + 1, j)
+                    if b == 0 and c + 1 == CHUNKS:
+                        quantise_x(1, j)
+                    project_and_rotate(b, c, j, plain, rotated)
+                is_key = c // (CHUNKS // 2)
+                first_head = (c % (CHUNKS // 2)) * HEADS
+                store(plain, (out_0, out_1)[is_key], b, first_head)
+                store(rotated, (out_2, out_3)[is_key], b, first_head)

@@ -18,11 +18,13 @@ P = 128
 PACK = 4
 PASSES = C // (P * PACK)
 J = T // P
-CHUNK = 512
-CHUNKS = 2 * C // CHUNK
-ROW_TILES = CHUNK // P
-HEADS = CHUNK // DH
+BANK = J * DH
+QK_HEADS = 2 * H
 PAIRS = DH // 2
+FLIP_AHEAD = 3
+QUANTISE_AHEAD = 2
+X_EVERY = QK_HEADS // J
+ADD_BANKS = 2
 
 FLOPS = 2 * B * T * C * 2 * C
 
@@ -37,30 +39,23 @@ def tile_ropeattnlayer_pa_kernel(tc, x, w_qk, out_0, out_1, out_2, out_3):
         loaded = ctx.enter_context(tc.tile_pool(name="loaded", bufs=1))
         keep = ctx.enter_context(tc.tile_pool(name="keep", bufs=1))
         stage = ctx.enter_context(tc.tile_pool(name="stage", bufs=4))
-        results = ctx.enter_context(tc.tile_pool(name="results", bufs=3))
+        work = ctx.enter_context(tc.tile_pool(name="work", bufs=3))
+        results = ctx.enter_context(tc.tile_pool(name="results", bufs=6))
         psum_flip = ctx.enter_context(tc.psum_pool(name="psum_flip", bufs=2))
         psum_acc = ctx.enter_context(tc.psum_pool(name="psum_acc", bufs=6))
+        ctx.enter_context(tc.manual_schedule())
 
-        w_tiles = w_qk.rearrange("(c t p) k -> c t p k", t=ROW_TILES, p=P)
+        w_tiles = w_qk.rearrange("(h p) k -> h p k", p=P)
         x_tiles = x.rearrange("b (p j) k -> b j p k", j=J)
-        w_rows = [[None] * ROW_TILES for c in range(CHUNKS)]
-        x_rows = [[None] * J for b in range(B)]
-
-        def load_w(c):
-            for t in range(ROW_TILES):
-                w_rows[c][t] = loaded.tile([P, C], BF16, name="w_rows%d_%d" % (c, t))
-                nc.sync.dma_start(out=w_rows[c][t][:], in_=w_tiles[c, t])
-
-        def load_x(b):
-            for j in range(J):
-                x_rows[b][j] = loaded.tile([P, C], BF16, name="x_rows%d_%d" % (b, j))
-                nc.sync.dma_start(out=x_rows[b][j][:], in_=x_tiles[b, j])
-
-        load_w(0)
-        load_x(0)
-        for c in range(1, CHUNKS):
-            load_w(c)
-        load_x(1)
+        w_rows = [loaded.tile([P, C], BF16, name="w_rows%d" % head) for head in range(QK_HEADS)]
+        x_rows = [[loaded.tile([P, C], BF16, name="x_rows%d_%d" % (b, j)) for j in range(J)] for b in range(B)]
+        nc.sync.dma_start(out=w_rows[0][:], in_=w_tiles[0])
+        for j in range(J):
+            nc.sync.dma_start(out=x_rows[0][j][:], in_=x_tiles[0, j])
+        for head in range(1, QK_HEADS):
+            nc.sync.dma_start(out=w_rows[head][:], in_=w_tiles[head])
+            if head % X_EVERY == X_EVERY - 1:
+                nc.sync.dma_start(out=x_rows[1][head // X_EVERY][:], in_=x_tiles[1, head // X_EVERY])
 
         zero = const.tile([P, 1], F32)
         nc.vector.memset(zero[:], 0.0)
@@ -73,17 +68,21 @@ def tile_ropeattnlayer_pa_kernel(tc, x, w_qk, out_0, out_1, out_2, out_3):
         masks.make_identity(nc, ident[:])
         position = const.tile([P, J], F32)
         nc.vector.tensor_copy(out=position[:], in_=position_int[:])
-        turns = const.tile([P, 2, J, PAIRS], F32)
-        nc.vector.tensor_scalar_mul(
-            out=turns[:, 1, :, 0:1], in0=position[:].unsqueeze(2), scalar1=RATIO / (2.0 * math.pi)
-        )
-        for doubling in range(6):
-            n = 2**doubling
+        turns = const.tile([P, 2, J, PAIRS, 2], F32)
+        for e in range(2):
             nc.vector.tensor_scalar_mul(
-                out=turns[:, 1, :, n : 2 * n], in0=turns[:, 1, :, 0:n], scalar1=RATIO**n
+                out=turns[:, 1, :, 0, e], in0=position[:], scalar1=(1 - 2 * e) * RATIO / (2.0 * math.pi)
             )
+        for level in range(3):
+            n = 4**level
+            for k in range(1, 4):
+                nc.vector.tensor_scalar_mul(
+                    out=turns[:, 1, :, k * n : (k + 1) * n, :],
+                    in0=turns[:, 1, :, 0:n, :],
+                    scalar1=RATIO ** (k * n),
+                )
         nc.vector.tensor_scalar_add(out=turns[:, 0], in0=turns[:, 1], scalar1=0.25)
-        whole = const.tile([P, 2, J, PAIRS], F32)
+        whole = const.tile([P, 2, J, PAIRS, 2], F32)
         nc.vector.tensor_scalar(
             out=whole[:],
             in0=turns[:],
@@ -92,27 +91,13 @@ def tile_ropeattnlayer_pa_kernel(tc, x, w_qk, out_0, out_1, out_2, out_3):
             op0=ALU.add,
             op1=ALU.subtract,
         )
-        part = const.tile([P, 2, J, PAIRS], F32)
+        part = const.tile([P, 2, J, PAIRS, 2], F32)
         nc.vector.tensor_sub(out=part[:], in0=turns[:], in1=whole[:])
-
-        table = const.tile([P, 2, J, DH], F32)
+        table = const.tile([P, 2, BANK], F32)
 
         def fill_table():
-            cos_part = part[:, 0].rearrange("p j i -> p (j i)")
-            sin_part = part[:, 1].rearrange("p j i -> p (j i)")
-            cos_out = table[:, 0].rearrange("p j (i e) -> p (j i) e", e=2)
-            sin_out = table[:, 1].rearrange("p j (i e) -> p (j i) e", e=2)
             nc.scalar.activation(
-                out=cos_out,
-                in_=cos_part.unsqueeze(2).to_broadcast([P, J * PAIRS, 2]),
-                func=ACT.Sin,
-                scale=2.0 * math.pi,
-            )
-            nc.scalar.activation(
-                out=sin_out[:, :, 0], in_=sin_part, func=ACT.Sin, scale=2.0 * math.pi
-            )
-            nc.scalar.activation(
-                out=sin_out[:, :, 1], in_=sin_part, func=ACT.Sin, scale=-2.0 * math.pi
+                out=table[:], in_=part[:].rearrange("p s j i e -> p s (j i e)"), func=ACT.Sin, scale=2.0 * math.pi
             )
 
         x_codes = [
@@ -124,13 +109,13 @@ def tile_ropeattnlayer_pa_kernel(tc, x, w_qk, out_0, out_1, out_2, out_3):
             for b in range(B)
         ]
         w_codes = [
-            keep.tile([P, PASSES, CHUNK], U32, name="w_codes%d" % c, align_bytes=64) for c in range(CHUNKS)
+            keep.tile([P, PASSES, P], U32, name="w_codes%d" % head, align_bytes=64) for head in range(QK_HEADS)
         ]
         w_scales = [
-            keep.tile([P, PASSES, CHUNK], U8, name="w_scales%d" % c, align_bytes=64) for c in range(CHUNKS)
+            keep.tile([P, PASSES, P], U8, name="w_scales%d" % head, align_bytes=64) for head in range(QK_HEADS)
         ]
 
-        def quantise_rows(rows, codes, scales):
+        def flip(rows):
             words = rows[:].bitcast(F32)
             flipped = psum_flip.tile([P, PASSES, 2, P], F32, tag="flipped")
             for g in range(PASSES):
@@ -142,72 +127,101 @@ def tile_ropeattnlayer_pa_kernel(tc, x, w_qk, out_0, out_1, out_2, out_3):
                 out=grouped[:].bitcast(F32).rearrange("p (g r u) -> p g r u", g=PASSES, u=2),
                 in_=flipped[:].rearrange("p g u r -> p g r u"),
             )
-            for g in range(PASSES):
-                nc.vector.quantize_mx(
-                    out=codes[:, g, :].bitcast(FP8X4),
-                    scales=scales[:, g, :],
-                    in_=grouped[:, g * P * PACK : (g + 1) * P * PACK],
-                )
+            return grouped
+
+        def quantise(grouped, codes, scales):
+            nc.vector.quantize_mx(
+                out=codes[:].rearrange("p g r -> p (g r)").bitcast(FP8X4),
+                scales=scales[:].rearrange("p g r -> p (g r)"),
+                in_=grouped[:],
+            )
+
+        grouped_x = {}
+        grouped_w = {}
+
+        def flip_x(b, j):
+            grouped_x[b, j] = flip(x_rows[b][j])
 
         def quantise_x(b, j):
-            quantise_rows(x_rows[b][j], x_codes[b][j][:], x_scales[b][j][:])
+            quantise(grouped_x[b, j], x_codes[b][j], x_scales[b][j])
 
-        def quantise_w(c, t):
-            columns = slice(t * P, (t + 1) * P)
-            quantise_rows(w_rows[c][t], w_codes[c][:, :, columns], w_scales[c][:, :, columns])
+        def flip_w(head):
+            grouped_w[head] = flip(w_rows[head])
 
-        def project_and_rotate(b, c, j, plain, rotated):
-            acc = psum_acc.tile([P, CHUNK], F32, tag="acc")
-            for g in range(PASSES):
-                nc.tensor.matmul_mx(
-                    out=acc[:],
-                    lhsT=x_codes[b][j][:, g, :].bitcast(FP8X4),
-                    lhsT_scale=x_scales[b][j][:, g, :],
-                    rhs=w_codes[c][:, g, :].bitcast(FP8X4),
-                    rhs_scale=w_scales[c][:, g, :],
-                    start=(g == 0),
-                    stop=(g == PASSES - 1),
-                )
-            by_head = acc[:].rearrange("p (h d) -> p h d", h=HEADS)
-            products = stage.tile([P, 2, HEADS, DH], F32, tag="products")
+        def quantise_w(head):
+            quantise(grouped_w[head], w_codes[head], w_scales[head])
+
+        def multiply(b, head):
+            acc = psum_acc.tile([P, BANK], F32, tag="acc")
+            for j in range(J):
+                for g in range(PASSES):
+                    nc.tensor.matmul_mx(
+                        out=acc[:, j * DH : (j + 1) * DH],
+                        lhsT=x_codes[b][j][:, g, :].bitcast(FP8X4),
+                        lhsT_scale=x_scales[b][j][:, g, :],
+                        rhs=w_codes[head][:, g, :].bitcast(FP8X4),
+                        rhs_scale=w_scales[head][:, g, :],
+                        start=(g == 0),
+                        stop=(g == PASSES - 1),
+                    )
+            return acc
+
+        def consume(acc, plain, products):
             nc.vector.tensor_tensor(
-                out=products[:],
-                in0=by_head.unsqueeze(1).to_broadcast([P, 2, HEADS, DH]),
-                in1=table[:, :, j, :].unsqueeze(2).to_broadcast([P, 2, HEADS, DH]),
-                op=ALU.mult,
+                out=products, in0=acc[:].unsqueeze(1).to_broadcast([P, 2, BANK]), in1=table[:], op=ALU.mult
             )
-            nc.scalar.copy(out=plain[:, :, j, :], in_=by_head)
-            pairs = "p h (i e) -> p h i e"
-            nc.gpsimd.tensor_tensor(
-                out=rotated[:, :, j, :].rearrange(pairs, e=2),
+            nc.scalar.copy(out=plain, in_=acc[:])
+
+        def rotate(engine, products, rotated):
+            pairs = "p h (n e) -> p (h n) e"
+            engine.tensor_tensor(
+                out=rotated[:].rearrange(pairs, e=2),
                 in0=products[:, 0].rearrange(pairs, e=2),
-                in1=products[:, 1].rearrange(pairs, e=2)[:, :, :, ::-1],
+                in1=products[:, 1].rearrange(pairs, e=2)[:, :, ::-1],
                 op=ALU.add,
             )
 
-        def store(result, out, b, first_head):
-            nc.sync.dma_start(
-                out=out[b, first_head : first_head + HEADS].rearrange("h (p j) d -> p h (j d)", j=J),
-                in_=result[:].rearrange("p h j d -> p h (j d)"),
+        def store(queue, result, out, b, first_head):
+            queue.dma_start(
+                out=out[b, first_head : first_head + ADD_BANKS].rearrange("h (p j) d -> p h (j d)", j=J),
+                in_=result[:],
             )
 
-        for t in range(ROW_TILES):
-            quantise_w(0, t)
-        quantise_x(0, 0)
+        flip_w(0)
+        quantise_w(0)
+        for j in range(J):
+            flip_x(0, j)
+            quantise_x(0, j)
         fill_table()
+        for head in range(1, FLIP_AHEAD):
+            flip_w(head)
+        for head in range(1, QUANTISE_AHEAD):
+            quantise_w(head)
+        acc_next = multiply(0, 0)
+
         for b in range(B):
-            for c in range(CHUNKS):
-                plain = results.tile([P, HEADS, J, DH], F32, tag="plain")
-                rotated = results.tile([P, HEADS, J, DH], F32, tag="rotated")
-                for j in range(J):
-                    if b == 0 and c == 0 and j + 1 < J:
-                        quantise_x(0, j + 1)
-                    if b == 0 and c + 1 < CHUNKS:
-                        quantise_w(c + 1, j)
-                    if b == 0 and c + 1 == CHUNKS:
-                        quantise_x(1, j)
-                    project_and_rotate(b, c, j, plain, rotated)
-                is_key = c // (CHUNKS // 2)
-                first_head = (c % (CHUNKS // 2)) * HEADS
-                store(plain, (out_0, out_1)[is_key], b, first_head)
-                store(rotated, (out_2, out_3)[is_key], b, first_head)
+            for head in range(QK_HEADS):
+                if b == 0 and head + FLIP_AHEAD < QK_HEADS:
+                    flip_w(head + FLIP_AHEAD)
+                if b == 0 and head % X_EVERY == 1:
+                    flip_x(1, head // X_EVERY)
+                acc = acc_next
+                following = b * QK_HEADS + head + 1
+                if following < B * QK_HEADS:
+                    acc_next = multiply(following // QK_HEADS, following % QK_HEADS)
+                n = head % ADD_BANKS
+                if n == 0:
+                    plain = results.tile([P, ADD_BANKS, BANK], F32, tag="plain")
+                    rotated = results.tile([P, ADD_BANKS, BANK], F32, tag="rotated")
+                    products = work.tile([P, 2, ADD_BANKS, BANK], F32, tag="products")
+                consume(acc, plain[:, n, :], products[:, :, n, :])
+                if b == 0 and head + QUANTISE_AHEAD < QK_HEADS:
+                    quantise_w(head + QUANTISE_AHEAD)
+                if b == 0 and head % X_EVERY == 2:
+                    quantise_x(1, head // X_EVERY)
+                if n == ADD_BANKS - 1:
+                    is_last = following == B * QK_HEADS
+                    rotate(nc.vector if is_last else nc.gpsimd, products, rotated)
+                    first_head = head - n
+                    store(nc.scalar, plain, (out_0, out_1)[first_head // H], b, first_head % H)
+                    store(nc.sync, rotated, (out_2, out_3)[first_head // H], b, first_head % H)

@@ -21,10 +21,10 @@ J = T // P
 BANK = J * DH
 QK_HEADS = 2 * H
 PAIRS = DH // 2
-FLIP_AHEAD = 3
-QUANTISE_AHEAD = 2
-X_EVERY = QK_HEADS // J
 ADD_BANKS = 2
+QUANTISE_AHEAD = 2
+FLIP_AHEAD = 4
+X_EVERY = QK_HEADS // J
 
 FLOPS = 2 * B * T * C * 2 * C
 
@@ -38,7 +38,7 @@ def tile_ropeattnlayer_pa_kernel(tc, x, w_qk, out_0, out_1, out_2, out_3):
         const = ctx.enter_context(tc.tile_pool(name="const", bufs=1))
         loaded = ctx.enter_context(tc.tile_pool(name="loaded", bufs=1))
         keep = ctx.enter_context(tc.tile_pool(name="keep", bufs=1))
-        stage = ctx.enter_context(tc.tile_pool(name="stage", bufs=4))
+        stage = ctx.enter_context(tc.tile_pool(name="stage", bufs=6))
         work = ctx.enter_context(tc.tile_pool(name="work", bufs=3))
         results = ctx.enter_context(tc.tile_pool(name="results", bufs=6))
         psum_flip = ctx.enter_context(tc.psum_pool(name="psum_flip", bufs=2))
@@ -115,7 +115,7 @@ def tile_ropeattnlayer_pa_kernel(tc, x, w_qk, out_0, out_1, out_2, out_3):
             keep.tile([P, PASSES, P], U8, name="w_scales%d" % head, align_bytes=64) for head in range(QK_HEADS)
         ]
 
-        def flip(rows):
+        def flip(rows, copy_out):
             words = rows[:].bitcast(F32)
             flipped = psum_flip.tile([P, PASSES, 2, P], F32, tag="flipped")
             for g in range(PASSES):
@@ -123,7 +123,7 @@ def tile_ropeattnlayer_pa_kernel(tc, x, w_qk, out_0, out_1, out_2, out_3):
                     first = (2 * g + u) * P
                     nc.tensor.transpose(flipped[:, g, u, :], words[:, first : first + P], ident[:])
             grouped = stage.tile([P, PASSES * P * PACK], BF16, tag="grouped", align_bytes=64)
-            nc.scalar.copy(
+            copy_out(
                 out=grouped[:].bitcast(F32).rearrange("p (g r u) -> p g r u", g=PASSES, u=2),
                 in_=flipped[:].rearrange("p g u r -> p g r u"),
             )
@@ -139,14 +139,14 @@ def tile_ropeattnlayer_pa_kernel(tc, x, w_qk, out_0, out_1, out_2, out_3):
         grouped_x = {}
         grouped_w = {}
 
-        def flip_x(b, j):
-            grouped_x[b, j] = flip(x_rows[b][j])
+        def flip_x(b, j, copy_out):
+            grouped_x[b, j] = flip(x_rows[b][j], copy_out)
 
         def quantise_x(b, j):
             quantise(grouped_x[b, j], x_codes[b][j], x_scales[b][j])
 
         def flip_w(head):
-            grouped_w[head] = flip(w_rows[head])
+            grouped_w[head] = flip(w_rows[head], nc.scalar.copy)
 
         def quantise_w(head):
             quantise(grouped_w[head], w_codes[head], w_scales[head])
@@ -181,47 +181,50 @@ def tile_ropeattnlayer_pa_kernel(tc, x, w_qk, out_0, out_1, out_2, out_3):
                 op=ALU.add,
             )
 
-        def store(queue, result, out, b, first_head):
-            queue.dma_start(
+        def store(result, out, b, first_head):
+            nc.sync.dma_start(
                 out=out[b, first_head : first_head + ADD_BANKS].rearrange("h (p j) d -> p h (j d)", j=J),
                 in_=result[:],
             )
 
         flip_w(0)
-        quantise_w(0)
-        for j in range(J):
-            flip_x(0, j)
-            quantise_x(0, j)
         fill_table()
-        for head in range(1, FLIP_AHEAD):
+        for j in range(J):
+            flip_x(0, j, nc.vector.tensor_copy)
+            quantise_x(0, j)
+        quantise_w(0)
+        for head in range(1, 1 + QUANTISE_AHEAD):
             flip_w(head)
-        for head in range(1, QUANTISE_AHEAD):
+        for head in range(1, 1 + QUANTISE_AHEAD):
             quantise_w(head)
         acc_next = multiply(0, 0)
+        for head in range(1 + QUANTISE_AHEAD, FLIP_AHEAD):
+            flip_w(head)
 
         for b in range(B):
             for head in range(QK_HEADS):
-                if b == 0 and head + FLIP_AHEAD < QK_HEADS:
-                    flip_w(head + FLIP_AHEAD)
-                if b == 0 and head % X_EVERY == 1:
-                    flip_x(1, head // X_EVERY)
                 acc = acc_next
                 following = b * QK_HEADS + head + 1
                 if following < B * QK_HEADS:
                     acc_next = multiply(following // QK_HEADS, following % QK_HEADS)
+                if b == 0 and head + FLIP_AHEAD < QK_HEADS:
+                    flip_w(head + FLIP_AHEAD)
+                if b == 0 and head % X_EVERY == 0:
+                    flip_x(1, head // X_EVERY, nc.scalar.copy)
                 n = head % ADD_BANKS
                 if n == 0:
                     plain = results.tile([P, ADD_BANKS, BANK], F32, tag="plain")
                     rotated = results.tile([P, ADD_BANKS, BANK], F32, tag="rotated")
                     products = work.tile([P, 2, ADD_BANKS, BANK], F32, tag="products")
                 consume(acc, plain[:, n, :], products[:, :, n, :])
-                if b == 0 and head + QUANTISE_AHEAD < QK_HEADS:
-                    quantise_w(head + QUANTISE_AHEAD)
-                if b == 0 and head % X_EVERY == 2:
-                    quantise_x(1, head // X_EVERY)
                 if n == ADD_BANKS - 1:
+                    first_head = head - n
+                    if b == 0:
+                        for later in range(head + QUANTISE_AHEAD, min(head + QUANTISE_AHEAD + ADD_BANKS, QK_HEADS)):
+                            quantise_w(later)
+                        if first_head % X_EVERY == 0:
+                            quantise_x(1, first_head // X_EVERY)
                     is_last = following == B * QK_HEADS
                     rotate(nc.vector if is_last else nc.gpsimd, products, rotated)
-                    first_head = head - n
-                    store(nc.scalar, plain, (out_0, out_1)[first_head // H], b, first_head % H)
-                    store(nc.sync, rotated, (out_2, out_3)[first_head // H], b, first_head % H)
+                    store(plain, (out_0, out_1)[first_head // H], b, first_head % H)
+                    store(rotated, (out_2, out_3)[first_head // H], b, first_head % H)

import math
from contextlib import ExitStack

import concourse.masks as masks
import concourse.mybir as mybir

F32 = mybir.dt.float32
BF16 = mybir.dt.bfloat16
I32 = mybir.dt.int32
U32 = mybir.dt.uint32
U8 = mybir.dt.uint8
FP8X4 = mybir.dt.float8_e4m3fn_x4
ALU = mybir.AluOpType
ACT = mybir.ActivationFunctionType

B, T, C, H, DH = 2, 512, 1024, 8, 128
P = 128
PACK = 4
PASSES = C // (P * PACK)
J = T // P
BANK = J * DH
QK_HEADS = 2 * H
PAIRS = DH // 2
ADD_BANKS = 2
QUANTISE_AHEAD = 2
FLIP_AHEAD = 4
X_EVERY = QK_HEADS // J

FLOPS = 2 * B * T * C * 2 * C

RATIO = 1000.0 ** (-2.0 / DH)
ROUND_MAGIC = 1.5 * 2.0**23


def tile_ropeattnlayer_pa_kernel(tc, x, w_qk, out_0, out_1, out_2, out_3):
    nc = tc.nc
    with ExitStack() as ctx:
        const = ctx.enter_context(tc.tile_pool(name="const", bufs=1))
        loaded = ctx.enter_context(tc.tile_pool(name="loaded", bufs=1))
        keep = ctx.enter_context(tc.tile_pool(name="keep", bufs=1))
        stage = ctx.enter_context(tc.tile_pool(name="stage", bufs=6))
        work = ctx.enter_context(tc.tile_pool(name="work", bufs=3))
        results = ctx.enter_context(tc.tile_pool(name="results", bufs=6))
        psum_flip = ctx.enter_context(tc.psum_pool(name="psum_flip", bufs=2))
        psum_acc = ctx.enter_context(tc.psum_pool(name="psum_acc", bufs=6))
        ctx.enter_context(tc.manual_schedule())

        w_tiles = w_qk.rearrange("(h p) k -> h p k", p=P)
        x_tiles = x.rearrange("b (p j) k -> b j p k", j=J)
        w_rows = [loaded.tile([P, C], BF16, name="w_rows%d" % head) for head in range(QK_HEADS)]
        x_rows = [[loaded.tile([P, C], BF16, name="x_rows%d_%d" % (b, j)) for j in range(J)] for b in range(B)]
        nc.sync.dma_start(out=w_rows[0][:], in_=w_tiles[0])
        for j in range(J):
            nc.sync.dma_start(out=x_rows[0][j][:], in_=x_tiles[0, j])
        for head in range(1, QK_HEADS):
            nc.sync.dma_start(out=w_rows[head][:], in_=w_tiles[head])
            if head % X_EVERY == X_EVERY - 1:
                nc.sync.dma_start(out=x_rows[1][head // X_EVERY][:], in_=x_tiles[1, head // X_EVERY])

        zero = const.tile([P, 1], F32)
        nc.vector.memset(zero[:], 0.0)
        warm = const.tile([P, 1], F32)
        nc.scalar.activation(out=warm[:], in_=zero[:], func=ACT.Sin)

        position_int = const.tile([P, J], I32)
        nc.gpsimd.iota(position_int[:], pattern=[[1, J]], base=1, channel_multiplier=J)
        ident = const.tile([P, P], F32)
        masks.make_identity(nc, ident[:])
        position = const.tile([P, J], F32)
        nc.vector.tensor_copy(out=position[:], in_=position_int[:])
        turns = const.tile([P, 2, J, PAIRS, 2], F32)
        for e in range(2):
            nc.vector.tensor_scalar_mul(
                out=turns[:, 1, :, 0, e], in0=position[:], scalar1=(1 - 2 * e) * RATIO / (2.0 * math.pi)
            )
        for level in range(3):
            n = 4**level
            for k in range(1, 4):
                nc.vector.tensor_scalar_mul(
                    out=turns[:, 1, :, k * n : (k + 1) * n, :],
                    in0=turns[:, 1, :, 0:n, :],
                    scalar1=RATIO ** (k * n),
                )
        nc.vector.tensor_scalar_add(out=turns[:, 0], in0=turns[:, 1], scalar1=0.25)
        whole = const.tile([P, 2, J, PAIRS, 2], F32)
        nc.vector.tensor_scalar(
            out=whole[:],
            in0=turns[:],
            scalar1=ROUND_MAGIC,
            scalar2=ROUND_MAGIC,
            op0=ALU.add,
            op1=ALU.subtract,
        )
        part = const.tile([P, 2, J, PAIRS, 2], F32)
        nc.vector.tensor_sub(out=part[:], in0=turns[:], in1=whole[:])
        table = const.tile([P, 2, BANK], F32)

        def fill_table():
            nc.scalar.activation(
                out=table[:], in_=part[:].rearrange("p s j i e -> p s (j i e)"), func=ACT.Sin, scale=2.0 * math.pi
            )

        x_codes = [
            [keep.tile([P, PASSES, P], U32, name="x_codes%d_%d" % (b, j), align_bytes=64) for j in range(J)]
            for b in range(B)
        ]
        x_scales = [
            [keep.tile([P, PASSES, P], U8, name="x_scales%d_%d" % (b, j), align_bytes=64) for j in range(J)]
            for b in range(B)
        ]
        w_codes = [
            keep.tile([P, PASSES, P], U32, name="w_codes%d" % head, align_bytes=64) for head in range(QK_HEADS)
        ]
        w_scales = [
            keep.tile([P, PASSES, P], U8, name="w_scales%d" % head, align_bytes=64) for head in range(QK_HEADS)
        ]

        def flip(rows, copy_out):
            words = rows[:].bitcast(F32)
            flipped = psum_flip.tile([P, PASSES, 2, P], F32, tag="flipped")
            for g in range(PASSES):
                for u in range(2):
                    first = (2 * g + u) * P
                    nc.tensor.transpose(flipped[:, g, u, :], words[:, first : first + P], ident[:])
            grouped = stage.tile([P, PASSES * P * PACK], BF16, tag="grouped", align_bytes=64)
            copy_out(
                out=grouped[:].bitcast(F32).rearrange("p (g r u) -> p g r u", g=PASSES, u=2),
                in_=flipped[:].rearrange("p g u r -> p g r u"),
            )
            return grouped

        def quantise(grouped, codes, scales):
            nc.vector.quantize_mx(
                out=codes[:].rearrange("p g r -> p (g r)").bitcast(FP8X4),
                scales=scales[:].rearrange("p g r -> p (g r)"),
                in_=grouped[:],
            )

        grouped_x = {}
        grouped_w = {}

        def flip_x(b, j, copy_out):
            grouped_x[b, j] = flip(x_rows[b][j], copy_out)

        def quantise_x(b, j):
            quantise(grouped_x[b, j], x_codes[b][j], x_scales[b][j])

        def flip_w(head):
            grouped_w[head] = flip(w_rows[head], nc.scalar.copy)

        def quantise_w(head):
            quantise(grouped_w[head], w_codes[head], w_scales[head])

        def multiply(b, head):
            acc = psum_acc.tile([P, BANK], F32, tag="acc")
            for j in range(J):
                for g in range(PASSES):
                    nc.tensor.matmul_mx(
                        out=acc[:, j * DH : (j + 1) * DH],
                        lhsT=x_codes[b][j][:, g, :].bitcast(FP8X4),
                        lhsT_scale=x_scales[b][j][:, g, :],
                        rhs=w_codes[head][:, g, :].bitcast(FP8X4),
                        rhs_scale=w_scales[head][:, g, :],
                        start=(g == 0),
                        stop=(g == PASSES - 1),
                    )
            return acc

        def consume(acc, plain, products):
            nc.vector.tensor_tensor(
                out=products, in0=acc[:].unsqueeze(1).to_broadcast([P, 2, BANK]), in1=table[:], op=ALU.mult
            )
            nc.scalar.copy(out=plain, in_=acc[:])

        def rotate(engine, products, rotated):
            pairs = "p h (n e) -> p (h n) e"
            engine.tensor_tensor(
                out=rotated[:].rearrange(pairs, e=2),
                in0=products[:, 0].rearrange(pairs, e=2),
                in1=products[:, 1].rearrange(pairs, e=2)[:, :, ::-1],
                op=ALU.add,
            )

        def store(result, out, b, first_head):
            nc.sync.dma_start(
                out=out[b, first_head : first_head + ADD_BANKS].rearrange("h (p j) d -> p h (j d)", j=J),
                in_=result[:],
            )

        flip_w(0)
        fill_table()
        for j in range(J):
            flip_x(0, j, nc.vector.tensor_copy)
            quantise_x(0, j)
        quantise_w(0)
        for head in range(1, 1 + QUANTISE_AHEAD):
            flip_w(head)
        for head in range(1, 1 + QUANTISE_AHEAD):
            quantise_w(head)
        acc_next = multiply(0, 0)
        for head in range(1 + QUANTISE_AHEAD, FLIP_AHEAD):
            flip_w(head)

        for b in range(B):
            for head in range(QK_HEADS):
                acc = acc_next
                following = b * QK_HEADS + head + 1
                if following < B * QK_HEADS:
                    acc_next = multiply(following // QK_HEADS, following % QK_HEADS)
                if b == 0 and head + FLIP_AHEAD < QK_HEADS:
                    flip_w(head + FLIP_AHEAD)
                if b == 0 and head % X_EVERY == 0:
                    flip_x(1, head // X_EVERY, nc.scalar.copy)
                n = head % ADD_BANKS
                if n == 0:
                    plain = results.tile([P, ADD_BANKS, BANK], F32, tag="plain")
                    rotated = results.tile([P, ADD_BANKS, BANK], F32, tag="rotated")
                    products = work.tile([P, 2, ADD_BANKS, BANK], F32, tag="products")
                consume(acc, plain[:, n, :], products[:, :, n, :])
                if n == ADD_BANKS - 1:
                    first_head = head - n
                    if b == 0:
                        for later in range(head + QUANTISE_AHEAD, min(head + QUANTISE_AHEAD + ADD_BANKS, QK_HEADS)):
                            quantise_w(later)
                        if first_head % X_EVERY == 0:
                            quantise_x(1, first_head // X_EVERY)
                    is_last = following == B * QK_HEADS
                    rotate(nc.vector if is_last else nc.gpsimd, products, rotated)
                    store(plain, (out_0, out_1)[first_head // H], b, first_head % H)
                    store(rotated, (out_2, out_3)[first_head // H], b, first_head % H)
